import numpy as np
import ml_dtypes


def mxq(x, axis, fmt="e4m3"):
    dtype, down = {"e4m3": (ml_dtypes.float8_e4m3fn, 7), "e5m2": (ml_dtypes.float8_e5m2, 14)}[fmt]
    v = np.moveaxis(np.asarray(x, np.float32).astype(ml_dtypes.bfloat16).astype(np.float64), axis, -1)
    blocks = v.reshape(v.shape[:-1] + (-1, 32))
    amax = np.abs(blocks).max(-1, keepdims=True)
    byte = np.maximum(np.where(amax > 0, np.frexp(amax)[1] - 1 + 127, 0) - down, 1)
    scale = np.exp2(byte - 127.0)
    codes = (blocks / scale).astype(np.float32).astype(dtype).astype(np.float64)
    return np.moveaxis((codes * scale).reshape(v.shape), -1, axis)


WIDE = False


def mx_kscale(k):
    if not WIDE:
        return np.ones(k)
    levels = np.array([10, -10, 5, -5, 0])
    a = np.random.permutation(np.resize(levels, k // 512 * 4)).reshape(k // 512, 4)
    idx = np.arange(k)
    return np.exp2(a[idx // 512, idx % 128 // 32])


BF16 = ml_dtypes.bfloat16


def bf(x):
    return np.asarray(x, np.float32).astype(BF16)


def f64(x):
    return np.asarray(x).astype(np.float64)


E2M1 = np.array([0.0, 0.5, 1.0, 1.5, 2.0, 3.0, 4.0, 6.0, -0.0, -0.5, -1.0, -1.5, -2.0, -3.0, -4.0, -6.0])


def pack_weight(w, fmt):
    k, n = w.shape
    w = f64(bf(w)).reshape(k // 32, 32, n)
    amax = np.abs(w).max(1)
    if fmt == "e4m3":
        byte = np.frexp(amax)[1] - 1 + 127 - 7
    else:
        mant, ex = np.frexp(amax / 6.0)
        byte = np.where(mant > 0.5, ex, ex - 1) + 127
    byte = np.clip(np.where(amax > 0, byte, 1), 1, 254)
    scaled = (w * np.exp2(127.0 - byte)[:, None, :]).reshape(k, n).astype(np.float32)
    by_word = np.ascontiguousarray(scaled.reshape(k // 512, 128, 4, n).transpose(0, 1, 3, 2))
    if fmt == "e4m3":
        words = by_word.astype(ml_dtypes.float8_e4m3fn).view(np.uint8)
    else:
        c = by_word.astype(ml_dtypes.float4_e2m1fn).view(np.uint8) & 0xF
        words = c[..., 0::2] | (c[..., 1::2] << 4)
    return np.ascontiguousarray(words), np.ascontiguousarray(byte.astype(np.uint8).reshape(k // 512, 16, n))


def unpack_weight(words, scales, fmt):
    g, p, n, _ = words.shape
    if fmt == "e4m3":
        vals = np.ascontiguousarray(words).view(ml_dtypes.float8_e4m3fn).astype(np.float64)
    else:
        nib = np.empty((g, p, n, 4), np.uint8)
        nib[..., 0::2] = words & 0xF
        nib[..., 1::2] = words >> 4
        vals = E2M1[nib]
    vals = vals * np.repeat(np.exp2(scales.astype(np.float64) - 127.0), 8, axis=1)[..., None]
    return vals.transpose(0, 1, 3, 2).reshape(g * 512, n)


B, R, CIN, N_CAPS, COUT = 256, 1152, 8, 16, 16
K = R * CIN


def squash(t, axis=-1):
    sq = np.sum(t * t, axis=axis, keepdims=True)
    return sq / (1.0 + sq) * t / np.sqrt(sq)


def setup_inputs():
    s = mx_kscale(K).reshape(R, CIN)
    x = np.random.standard_normal((B, R, CIN)) * s
    W = np.random.standard_normal((N_CAPS, R, CIN, COUT)) * np.sqrt(3.0 * R / (CIN * COUT)) / s[:, :, None]
    cat = W.reshape(N_CAPS, K, COUT).reshape(-1, COUT)
    words, scales = pack_weight(cat, "e4m3")
    return {"x": bf(x), "W_words": words, "W_scales": scales}


def reference(x, W_words, W_scales):
    xq = mxq(f64(x).reshape(B, K), 1, "e4m3")
    wq = unpack_weight(W_words, W_scales, "e4m3").reshape(N_CAPS, K, COUT)
    c = 1.0 / R
    s = (c * (xq @ wq))[:, :, None, :]
    v = squash(s, axis=-1)
    return v[:, :, :, None, :]

@@ -1,0 +1,146 @@
+import concourse.masks as masks
+import concourse.mybir as mybir
+
+F32 = mybir.dt.float32
+BF16 = mybir.dt.bfloat16
+I32 = mybir.dt.int32
+U32 = mybir.dt.uint32
+U8 = mybir.dt.uint8
+FP8X4 = mybir.dt.float8_e4m3fn_x4
+ACT = mybir.ActivationFunctionType
+ALU = mybir.AluOpType
+AXIS = mybir.AxisListType
+
+BATCH, ROUTES, C_IN, CAPS, C_OUT = 256, 1152, 8, 16, 16
+K = ROUTES * C_IN
+P = 128
+PACK = 4
+K_PASS = P * PACK
+PASSES = K // K_PASS
+HALVES = BATCH // P
+COLS = CAPS * C_OUT
+PAIRS = PACK // 2
+CHUNK_PASSES = 3
+CHUNKS = PASSES // CHUNK_PASSES
+CHUNK_K = CHUNK_PASSES * K_PASS
+BLOCKS = K_PASS // 32
+SCALE_WORDS = C_OUT // 4
+ROWS_PER_CHUNK = -(-BLOCKS // CHUNKS)
+
+FLOPS = 2 * BATCH * K * COLS
+
+
+def tile_capsulelayer_e_kernel(tc, x, W_words, W_scales, out):
+    nc = tc.nc
+    x_rows = x.rearrange("(h b) r i -> b h (r i)", b=P)
+    w_by_pass = W_words.rearrange("(e g) p o t -> g p e (o t)", g=PASSES)
+    scale_rows = W_scales.rearrange("c q o -> q c o")
+    out_rows = out.rearrange("e (h b) y z o -> h b e (y z o)", b=P)
+
+    with tc.manual_schedule(), tc.tile_pool(name="keep", bufs=1) as keep, tc.tile_pool(
+        name="x_in", bufs=CHUNKS
+    ) as x_in, tc.tile_pool(name="by_pass", bufs=PASSES) as by_pass, tc.tile_pool(
+        name="stage", bufs=3
+    ) as stage, tc.tile_pool(name="squash", bufs=HALVES) as squash, tc.psum_pool(
+        name="flipped", bufs=4
+    ) as flipped, tc.psum_pool(name="sums", bufs=HALVES) as sums:
+        w_scales_in = keep.tile([P, CAPS * PASSES * C_OUT], U8, align_bytes=64)
+        nc.vector.memset(w_scales_in[:].bitcast(I32), 0)
+        one = keep.tile([P, 1], F32)
+        nc.vector.memset(one[:], 1.0)
+        warm = keep.tile([P, 1], F32)
+        nc.scalar.activation(out=warm[:], in_=one[:], func=ACT.Sqrt)
+        ident = keep.tile([P, P], F32)
+        masks.make_identity(nc, ident[:])
+
+        x_chunks = []
+        for c in range(CHUNKS):
+            x_sb = x_in.tile([P, HALVES, CHUNK_K], BF16)
+            nc.scalar.dma_start(out=x_sb[:], in_=x_rows[:, :, c * CHUNK_K : (c + 1) * CHUNK_K])
+            x_chunks.append(x_sb)
+            for q in range(c * ROWS_PER_CHUNK, min((c + 1) * ROWS_PER_CHUNK, BLOCKS)):
+                row = 32 * (q // 4) + q % 4
+                nc.sync.dma_start(
+                    out=w_scales_in[row : row + 1, :].bitcast(I32).rearrange("r (c w) -> r c w", w=SCALE_WORDS),
+                    in_=scale_rows[q : q + 1].bitcast(I32),
+                )
+        w_words = []
+        for g in range(PASSES):
+            w_sb = by_pass.tile([P, COLS * PACK], U8, align_bytes=64)
+            nc.sync.dma_start(
+                out=w_sb[:].bitcast(I32).rearrange("p (e w) -> p e w", e=CAPS),
+                in_=w_by_pass[g].bitcast(I32),
+            )
+            w_words.append(w_sb)
+
+        x_codes = []
+        x_planes = []
+        for g in range(PASSES):
+            x_pairs = x_chunks[g // CHUNK_PASSES][:].bitcast(F32)
+            first = (g % CHUNK_PASSES) * (K_PASS // 2)
+            x_t = flipped.tile([P, HALVES, PAIRS, P], F32)
+            for h in range(HALVES):
+                for u in range(PAIRS):
+                    nc.tensor.transpose(
+                        x_t[:, h, u, :], x_pairs[:, h, first + u : first + K_PASS // 2 : PAIRS], ident[:]
+                    )
+            grouped = stage.tile([P, BATCH * PACK], BF16, align_bytes=64)
+            nc.scalar.copy(
+                out=grouped[:].bitcast(F32).rearrange("p (h b u) -> p h b u", h=HALVES, u=PAIRS),
+                in_=x_t[:].rearrange("p h u b -> p h b u"),
+            )
+            codes = by_pass.tile([P, BATCH], U32, align_bytes=64)
+            plane = by_pass.tile([P, BATCH], U8, align_bytes=64)
+            nc.vector.quantize_mx(out=codes[:].bitcast(FP8X4), scales=plane[:], in_=grouped[:])
+            x_codes.append(codes)
+            x_planes.append(plane)
+
+        w_planes = keep.tile([P, PASSES, COLS], U8, align_bytes=64)
+        nc.vector.tensor_copy(
+            out=w_planes[:].rearrange("p g c -> p (g c)").bitcast(I32).rearrange(
+                "p (g e w) -> p g e w", g=PASSES, e=CAPS
+            ),
+            in_=w_scales_in[:].bitcast(I32).rearrange("p (e g w) -> p g e w", e=CAPS, g=PASSES),
+        )
+
+        acc = []
+        for h in range(HALVES):
+            acc_h = sums.tile([P, CAPS, C_OUT], F32)
+            acc.append(acc_h)
+        for g in range(PASSES):
+            for h in range(HALVES):
+                rows = slice(h * P, (h + 1) * P)
+                nc.tensor.matmul_mx(
+                    out=acc[h][:].rearrange("p e o -> p (e o)"),
+                    lhsT=x_codes[g][:, rows].bitcast(FP8X4),
+                    lhsT_scale=x_planes[g][:, rows],
+                    rhs=w_words[g][:].bitcast(FP8X4),
+                    rhs_scale=w_planes[:, g, :],
+                    start=(g == 0),
+                    stop=(g == PASSES - 1),
+                )
+
+        squares = squash.tile([P, HALVES, CAPS, C_OUT], F32)
+        sq = squash.tile([P, HALVES, CAPS], F32)
+        for h in range(HALVES):
+            nc.scalar.activation(out=squares[:, h], in_=acc[h][:], func=ACT.Square, scale=1.0 / ROUTES)
+            nc.vector.tensor_reduce(out=sq[:, h, :], in_=squares[:, h], axis=AXIS.X, op=ALU.add)
+        root = squash.tile([P, HALVES, CAPS], F32)
+        nc.scalar.activation(out=root[:], in_=sq[:], func=ACT.Sqrt)
+        one_plus_sq = squash.tile([P, HALVES, CAPS], F32)
+        nc.vector.tensor_scalar_add(one_plus_sq[:], sq[:], 1.0)
+        inverse = squash.tile([P, HALVES, CAPS], F32)
+        nc.vector.reciprocal(inverse[:], one_plus_sq[:])
+        factor = squash.tile([P, HALVES, CAPS], F32)
+        nc.vector.scalar_tensor_tensor(
+            out=factor[:], in0=root[:], scalar=1.0 / ROUTES, in1=inverse[:], op0=ALU.mult, op1=ALU.mult
+        )
+        for h in range(HALVES):
+            v = squash.tile([P, CAPS, C_OUT], F32)
+            nc.vector.tensor_tensor(
+                out=v[:],
+                in0=acc[h][:],
+                in1=factor[:, h, :].unsqueeze(2).to_broadcast([P, CAPS, C_OUT]),
+                op=ALU.mult,
+            )
+            nc.sync.dma_start(out=out_rows[h], in_=v[:])

@@ -25,7 +25,7 @@ CHUNKS = PASSES // CHUNK_PASSES
 CHUNK_K = CHUNK_PASSES * K_PASS
 BLOCKS = K_PASS // 32
 SCALE_WORDS = C_OUT // 4
-ROWS_PER_CHUNK = -(-BLOCKS // CHUNKS)
+QUADRANTS = 4
 
 FLOPS = 2 * BATCH * K * COLS
 
@@ -34,7 +34,7 @@ def tile_capsulelayer_e_kernel(tc, x, W_words, W_scales, out):
     nc = tc.nc
     x_rows = x.rearrange("(h b) r i -> b h (r i)", b=P)
     w_by_pass = W_words.rearrange("(e g) p o t -> g p e (o t)", g=PASSES)
-    scale_rows = W_scales.rearrange("c q o -> q c o")
+    scale_rows = W_scales.rearrange("c (q r) o -> q r c o", q=QUADRANTS)
     out_rows = out.rearrange("e (h b) y z o -> h b e (y z o)", b=P)
 
     with tc.manual_schedule(), tc.tile_pool(name="keep", bufs=1) as keep, tc.tile_pool(
@@ -53,17 +53,16 @@ def tile_capsulelayer_e_kernel(tc, x, W_words, W_scales, out):
         ident = keep.tile([P, P], F32)
         masks.make_identity(nc, ident[:])
 
+        for q in range(QUADRANTS):
+            nc.sync.dma_start(
+                out=w_scales_in[32 * q : 32 * q + 4, :].bitcast(I32).rearrange("r (c w) -> r c w", w=SCALE_WORDS),
+                in_=scale_rows[q].bitcast(I32),
+            )
         x_chunks = []
         for c in range(CHUNKS):
             x_sb = x_in.tile([P, HALVES, CHUNK_K], BF16)
             nc.scalar.dma_start(out=x_sb[:], in_=x_rows[:, :, c * CHUNK_K : (c + 1) * CHUNK_K])
             x_chunks.append(x_sb)
-            for q in range(c * ROWS_PER_CHUNK, min((c + 1) * ROWS_PER_CHUNK, BLOCKS)):
-                row = 32 * (q // 4) + q % 4
-                nc.sync.dma_start(
-                    out=w_scales_in[row : row + 1, :].bitcast(I32).rearrange("r (c w) -> r c w", w=SCALE_WORDS),
-                    in_=scale_rows[q : q + 1].bitcast(I32),
-                )
         w_words = []
         for g in range(PASSES):
             w_sb = by_pass.tile([P, COLS * PACK], U8, align_bytes=64)

@@ -25,7 +25,7 @@ CHUNKS = PASSES // CHUNK_PASSES
 CHUNK_K = CHUNK_PASSES * K_PASS
 BLOCKS = K_PASS // 32
 SCALE_WORDS = C_OUT // 4
-QUADRANTS = 4
+ROWS_PER_CHUNK = -(-BLOCKS // CHUNKS)
 
 FLOPS = 2 * BATCH * K * COLS
 
@@ -34,7 +34,7 @@ def tile_capsulelayer_e_kernel(tc, x, W_words, W_scales, out):
     nc = tc.nc
     x_rows = x.rearrange("(h b) r i -> b h (r i)", b=P)
     w_by_pass = W_words.rearrange("(e g) p o t -> g p e (o t)", g=PASSES)
-    scale_rows = W_scales.rearrange("c (q r) o -> q r c o", q=QUADRANTS)
+    scale_rows = W_scales.rearrange("c q o -> q c o")
     out_rows = out.rearrange("e (h b) y z o -> h b e (y z o)", b=P)
 
     with tc.manual_schedule(), tc.tile_pool(name="keep", bufs=1) as keep, tc.tile_pool(
@@ -53,23 +53,30 @@ def tile_capsulelayer_e_kernel(tc, x, W_words, W_scales, out):
         ident = keep.tile([P, P], F32)
         masks.make_identity(nc, ident[:])
 
-        for q in range(QUADRANTS):
-            nc.sync.dma_start(
-                out=w_scales_in[32 * q : 32 * q + 4, :].bitcast(I32).rearrange("r (c w) -> r c w", w=SCALE_WORDS),
-                in_=scale_rows[q].bitcast(I32),
-            )
         x_chunks = []
         for c in range(CHUNKS):
             x_sb = x_in.tile([P, HALVES, CHUNK_K], BF16)
             nc.scalar.dma_start(out=x_sb[:], in_=x_rows[:, :, c * CHUNK_K : (c + 1) * CHUNK_K])
             x_chunks.append(x_sb)
+            for q in range(c * ROWS_PER_CHUNK, min((c + 1) * ROWS_PER_CHUNK, BLOCKS)):
+                row = 32 * (q // 4) + q % 4
+                nc.sync.dma_start(
+                    out=w_scales_in[row : row + 1, :].bitcast(I32).rearrange("r (c w) -> r c w", w=SCALE_WORDS),
+                    in_=scale_rows[q : q + 1].bitcast(I32),
+                )
         w_words = []
         for g in range(PASSES):
             w_sb = by_pass.tile([P, COLS * PACK], U8, align_bytes=64)
-            nc.sync.dma_start(
-                out=w_sb[:].bitcast(I32).rearrange("p (e w) -> p e w", e=CAPS),
-                in_=w_by_pass[g].bitcast(I32),
-            )
+            if g % 2 == 0:
+                nc.sync.dma_start(
+                    out=w_sb[:].bitcast(I32).rearrange("p (e w) -> p e w", e=CAPS),
+                    in_=w_by_pass[g].bitcast(I32),
+                )
+            else:
+                nc.scalar.dma_start(
+                    out=w_sb[:].bitcast(F32).rearrange("p (e w) -> p e w", e=CAPS),
+                    in_=w_by_pass[g].bitcast(F32),
+                )
             w_words.append(w_sb)
 
         x_codes = []
@@ -84,7 +91,7 @@ def tile_capsulelayer_e_kernel(tc, x, W_words, W_scales, out):
                         x_t[:, h, u, :], x_pairs[:, h, first + u : first + K_PASS // 2 : PAIRS], ident[:]
                     )
             grouped = stage.tile([P, BATCH * PACK], BF16, align_bytes=64)
-            nc.scalar.copy(
+            nc.vector.tensor_copy(
                 out=grouped[:].bitcast(F32).rearrange("p (h b u) -> p h b u", h=HALVES, u=PAIRS),
                 in_=x_t[:].rearrange("p h u b -> p h b u"),
             )

@@ -18,7 +18,9 @@ PACK = 4
 K_PASS = P * PACK
 PASSES = K // K_PASS
 HALVES = BATCH // P
-COLS = CAPS * C_OUT
+GROUPS = 2
+GROUP_CAPS = CAPS // GROUPS
+GROUP_COLS = GROUP_CAPS * C_OUT
 PAIRS = PACK // 2
 CHUNK_PASSES = 3
 CHUNKS = PASSES // CHUNK_PASSES
@@ -27,23 +29,25 @@ BLOCKS = K_PASS // 32
 SCALE_WORDS = C_OUT // 4
 ROWS_PER_CHUNK = -(-BLOCKS // CHUNKS)
 
-FLOPS = 2 * BATCH * K * COLS
+FLOPS = 2 * BATCH * K * CAPS * C_OUT
 
 
 def tile_capsulelayer_e_kernel(tc, x, W_words, W_scales, out):
     nc = tc.nc
     x_rows = x.rearrange("(h b) r i -> b h (r i)", b=P)
-    w_by_pass = W_words.rearrange("(e g) p o t -> g p e (o t)", g=PASSES)
+    w_by_capsule = W_words.rearrange("(e g) p o t -> e p g (o t)", g=PASSES)
     scale_rows = W_scales.rearrange("c q o -> q c o")
     out_rows = out.rearrange("e (h b) y z o -> h b e (y z o)", b=P)
 
     with tc.manual_schedule(), tc.tile_pool(name="keep", bufs=1) as keep, tc.tile_pool(
         name="x_in", bufs=CHUNKS
     ) as x_in, tc.tile_pool(name="by_pass", bufs=PASSES) as by_pass, tc.tile_pool(
-        name="stage", bufs=3
-    ) as stage, tc.tile_pool(name="squash", bufs=HALVES) as squash, tc.psum_pool(
-        name="flipped", bufs=4
-    ) as flipped, tc.psum_pool(name="sums", bufs=HALVES) as sums:
+        name="by_group", bufs=GROUPS
+    ) as by_group, tc.tile_pool(name="stage", bufs=3) as stage, tc.tile_pool(
+        name="results", bufs=GROUPS * HALVES
+    ) as results, tc.psum_pool(name="flipped", bufs=4) as flipped, tc.psum_pool(
+        name="sums", bufs=GROUPS * HALVES
+    ) as sums:
         w_scales_in = keep.tile([P, CAPS * PASSES * C_OUT], U8, align_bytes=64)
         nc.vector.memset(w_scales_in[:].bitcast(I32), 0)
         one = keep.tile([P, 1], F32)
@@ -65,18 +69,10 @@ def tile_capsulelayer_e_kernel(tc, x, W_words, W_scales, out):
                     in_=scale_rows[q : q + 1].bitcast(I32),
                 )
         w_words = []
-        for g in range(PASSES):
-            w_sb = by_pass.tile([P, COLS * PACK], U8, align_bytes=64)
-            if g % 2 == 0:
-                nc.sync.dma_start(
-                    out=w_sb[:].bitcast(I32).rearrange("p (e w) -> p e w", e=CAPS),
-                    in_=w_by_pass[g].bitcast(I32),
-                )
-            else:
-                nc.scalar.dma_start(
-                    out=w_sb[:].bitcast(F32).rearrange("p (e w) -> p e w", e=CAPS),
-                    in_=w_by_pass[g].bitcast(F32),
-                )
+        for a in range(GROUPS):
+            w_sb = by_group.tile([P, PASSES, GROUP_CAPS, C_OUT * PACK], U8, align_bytes=64)
+            for j in range(GROUP_CAPS):
+                nc.sync.dma_start(out=w_sb[:, :, j, :].bitcast(I32), in_=w_by_capsule[a * GROUP_CAPS + j].bitcast(I32))
             w_words.append(w_sb)
 
         x_codes = []
@@ -91,7 +87,7 @@ def tile_capsulelayer_e_kernel(tc, x, W_words, W_scales, out):
                         x_t[:, h, u, :], x_pairs[:, h, first + u : first + K_PASS // 2 : PAIRS], ident[:]
                     )
             grouped = stage.tile([P, BATCH * PACK], BF16, align_bytes=64)
-            nc.vector.tensor_copy(
+            nc.scalar.copy(
                 out=grouped[:].bitcast(F32).rearrange("p (h b u) -> p h b u", h=HALVES, u=PAIRS),
                 in_=x_t[:].rearrange("p h u b -> p h b u"),
             )
@@ -101,52 +97,63 @@ def tile_capsulelayer_e_kernel(tc, x, W_words, W_scales, out):
             x_codes.append(codes)
             x_planes.append(plane)
 
-        w_planes = keep.tile([P, PASSES, COLS], U8, align_bytes=64)
-        nc.vector.tensor_copy(
-            out=w_planes[:].rearrange("p g c -> p (g c)").bitcast(I32).rearrange(
-                "p (g e w) -> p g e w", g=PASSES, e=CAPS
-            ),
-            in_=w_scales_in[:].bitcast(I32).rearrange("p (e g w) -> p g e w", e=CAPS, g=PASSES),
+        scales_in_words = w_scales_in[:].bitcast(I32).rearrange(
+            "p (a j g w) -> p a g j w", a=GROUPS, j=GROUP_CAPS, g=PASSES
         )
-
-        acc = []
-        for h in range(HALVES):
-            acc_h = sums.tile([P, CAPS, C_OUT], F32)
-            acc.append(acc_h)
-        for g in range(PASSES):
-            for h in range(HALVES):
-                rows = slice(h * P, (h + 1) * P)
-                nc.tensor.matmul_mx(
-                    out=acc[h][:].rearrange("p e o -> p (e o)"),
-                    lhsT=x_codes[g][:, rows].bitcast(FP8X4),
-                    lhsT_scale=x_planes[g][:, rows],
-                    rhs=w_words[g][:].bitcast(FP8X4),
-                    rhs_scale=w_planes[:, g, :],
-                    start=(g == 0),
-                    stop=(g == PASSES - 1),
-                )
-
-        squares = squash.tile([P, HALVES, CAPS, C_OUT], F32)
-        sq = squash.tile([P, HALVES, CAPS], F32)
-        for h in range(HALVES):
-            nc.scalar.activation(out=squares[:, h], in_=acc[h][:], func=ACT.Square, scale=1.0 / ROUTES)
-            nc.vector.tensor_reduce(out=sq[:, h, :], in_=squares[:, h], axis=AXIS.X, op=ALU.add)
-        root = squash.tile([P, HALVES, CAPS], F32)
-        nc.scalar.activation(out=root[:], in_=sq[:], func=ACT.Sqrt)
-        one_plus_sq = squash.tile([P, HALVES, CAPS], F32)
-        nc.vector.tensor_scalar_add(one_plus_sq[:], sq[:], 1.0)
-        inverse = squash.tile([P, HALVES, CAPS], F32)
-        nc.vector.reciprocal(inverse[:], one_plus_sq[:])
-        factor = squash.tile([P, HALVES, CAPS], F32)
-        nc.vector.scalar_tensor_tensor(
-            out=factor[:], in0=root[:], scalar=1.0 / ROUTES, in1=inverse[:], op0=ALU.mult, op1=ALU.mult
-        )
-        for h in range(HALVES):
-            v = squash.tile([P, CAPS, C_OUT], F32)
-            nc.vector.tensor_tensor(
-                out=v[:],
-                in0=acc[h][:],
-                in1=factor[:, h, :].unsqueeze(2).to_broadcast([P, CAPS, C_OUT]),
-                op=ALU.mult,
+        w_planes = []
+        for a in range(GROUPS):
+            planes = by_group.tile([P, PASSES, GROUP_COLS], U8, align_bytes=64)
+            nc.vector.tensor_copy(
+                out=planes[:].rearrange("p g c -> p (g c)").bitcast(I32).rearrange(
+                    "p (g j w) -> p g j w", g=PASSES, j=GROUP_CAPS
+                ),
+                in_=scales_in_words[:, a],
             )
-            nc.sync.dma_start(out=out_rows[h], in_=v[:])
+            w_planes.append(planes)
+
+        stores = []
+        for a in range(GROUPS):
+            acc = []
+            for h in range(HALVES):
+                acc_h = sums.tile([P, GROUP_CAPS, C_OUT], F32)
+                acc.append(acc_h)
+            for g in range(PASSES):
+                for h in range(HALVES):
+                    rows = slice(h * P, (h + 1) * P)
+                    nc.tensor.matmul_mx(
+                        out=acc[h][:].rearrange("p j o -> p (j o)"),
+                        lhsT=x_codes[g][:, rows].bitcast(FP8X4),
+                        lhsT_scale=x_planes[g][:, rows],
+                        rhs=w_words[a][:, g].rearrange("p j c -> p (j c)").bitcast(FP8X4),
+                        rhs_scale=w_planes[a][:, g, :],
+                        start=(g == 0),
+                        stop=(g == PASSES - 1),
+                    )
+
+            squares = by_group.tile([P, HALVES, GROUP_CAPS, C_OUT], F32)
+            sq = by_group.tile([P, HALVES, GROUP_CAPS], F32)
+            for h in range(HALVES):
+                nc.scalar.activation(out=squares[:, h], in_=acc[h][:], func=ACT.Square, scale=1.0 / ROUTES)
+                nc.vector.tensor_reduce(out=sq[:, h, :], in_=squares[:, h], axis=AXIS.X, op=ALU.add)
+            root = by_group.tile([P, HALVES, GROUP_CAPS], F32)
+            nc.scalar.activation(out=root[:], in_=sq[:], func=ACT.Sqrt)
+            one_plus_sq = by_group.tile([P, HALVES, GROUP_CAPS], F32)
+            nc.vector.tensor_scalar_add(one_plus_sq[:], sq[:], 1.0)
+            inverse = by_group.tile([P, HALVES, GROUP_CAPS], F32)
+            nc.vector.reciprocal(inverse[:], one_plus_sq[:])
+            factor = by_group.tile([P, HALVES, GROUP_CAPS], F32)
+            nc.vector.scalar_tensor_tensor(
+                out=factor[:], in0=root[:], scalar=1.0 / ROUTES, in1=inverse[:], op0=ALU.mult, op1=ALU.mult
+            )
+            for h in range(HALVES):
+                v = results.tile([P, GROUP_CAPS, C_OUT], F32)
+                nc.vector.tensor_tensor(
+                    out=v[:],
+                    in0=acc[h][:],
+                    in1=factor[:, h, :].unsqueeze(2).to_broadcast([P, GROUP_CAPS, C_OUT]),
+                    op=ALU.mult,
+                )
+                stores.append((out_rows[h][:, a * GROUP_CAPS : (a + 1) * GROUP_CAPS, :], v))
+
+        for rows_of_out, v in stores:
+            nc.sync.dma_start(out=rows_of_out, in_=v[:])

@@ -28,6 +28,8 @@ CHUNK_K = CHUNK_PASSES * K_PASS
 BLOCKS = K_PASS // 32
 SCALE_WORDS = C_OUT // 4
 ROWS_PER_CHUNK = -(-BLOCKS // CHUNKS)
+SHARED = 4
+SLOTS = GROUPS * PASSES // SHARED
 
 FLOPS = 2 * BATCH * K * CAPS * C_OUT
 
@@ -35,20 +37,22 @@ FLOPS = 2 * BATCH * K * CAPS * C_OUT
 def tile_capsulelayer_e_kernel(tc, x, W_words, W_scales, out):
     nc = tc.nc
     x_rows = x.rearrange("(h b) r i -> b h (r i)", b=P)
-    w_by_capsule = W_words.rearrange("(e g) p o t -> e p g (o t)", g=PASSES)
-    scale_rows = W_scales.rearrange("c q o -> q c o")
+    w_by_pass = W_words.rearrange("(j a g) p o t -> a g p j (o t)", a=GROUPS, g=PASSES)
+    scale_rows = W_scales.rearrange("(s i) q o -> q i s o", i=SHARED)
     out_rows = out.rearrange("e (h b) y z o -> h b e (y z o)", b=P)
 
     with tc.manual_schedule(), tc.tile_pool(name="keep", bufs=1) as keep, tc.tile_pool(
         name="x_in", bufs=CHUNKS
     ) as x_in, tc.tile_pool(name="by_pass", bufs=PASSES) as by_pass, tc.tile_pool(
         name="by_group", bufs=GROUPS
-    ) as by_group, tc.tile_pool(name="stage", bufs=3) as stage, tc.tile_pool(
+    ) as by_group, tc.tile_pool(name="operands", bufs=GROUPS * PASSES) as operands, tc.tile_pool(
+        name="stage", bufs=3
+    ) as stage, tc.tile_pool(
         name="results", bufs=GROUPS * HALVES
     ) as results, tc.psum_pool(name="flipped", bufs=4) as flipped, tc.psum_pool(
         name="sums", bufs=GROUPS * HALVES
     ) as sums:
-        w_scales_in = keep.tile([P, CAPS * PASSES * C_OUT], U8, align_bytes=64)
+        w_scales_in = keep.tile([P, CAPS * PASSES // SHARED * C_OUT], U8, align_bytes=64)
         nc.vector.memset(w_scales_in[:].bitcast(I32), 0)
         one = keep.tile([P, 1], F32)
         nc.vector.memset(one[:], 1.0)
@@ -65,15 +69,17 @@ def tile_capsulelayer_e_kernel(tc, x, W_words, W_scales, out):
             for q in range(c * ROWS_PER_CHUNK, min((c + 1) * ROWS_PER_CHUNK, BLOCKS)):
                 row = 32 * (q // 4) + q % 4
                 nc.sync.dma_start(
-                    out=w_scales_in[row : row + 1, :].bitcast(I32).rearrange("r (c w) -> r c w", w=SCALE_WORDS),
-                    in_=scale_rows[q : q + 1].bitcast(I32),
+                    out=w_scales_in[row : row + 4 * SHARED : 4, :].bitcast(I32).rearrange(
+                        "i (s w) -> i s w", w=SCALE_WORDS
+                    ),
+                    in_=scale_rows[q].bitcast(I32),
                 )
         w_words = []
         for a in range(GROUPS):
-            w_sb = by_group.tile([P, PASSES, GROUP_CAPS, C_OUT * PACK], U8, align_bytes=64)
-            for j in range(GROUP_CAPS):
-                nc.sync.dma_start(out=w_sb[:, :, j, :].bitcast(I32), in_=w_by_capsule[a * GROUP_CAPS + j].bitcast(I32))
-            w_words.append(w_sb)
+            for g in range(PASSES):
+                w_sb = operands.tile([P, GROUP_CAPS, C_OUT * PACK], U8, align_bytes=64)
+                nc.sync.dma_start(out=w_sb[:].bitcast(I32), in_=w_by_pass[a, g].bitcast(I32))
+                w_words.append(w_sb)
 
         x_codes = []
         x_planes = []
@@ -97,19 +103,13 @@ def tile_capsulelayer_e_kernel(tc, x, W_words, W_scales, out):
             x_codes.append(codes)
             x_planes.append(plane)
 
-        scales_in_words = w_scales_in[:].bitcast(I32).rearrange(
-            "p (a j g w) -> p a g j w", a=GROUPS, j=GROUP_CAPS, g=PASSES
+        w_planes = keep.tile([P, SLOTS, GROUP_COLS], U8, align_bytes=64)
+        nc.vector.tensor_copy(
+            out=w_planes[:].rearrange("p s c -> p (s c)").bitcast(I32).rearrange(
+                "p (s j w) -> p s j w", s=SLOTS, j=GROUP_CAPS
+            ),
+            in_=w_scales_in[:].bitcast(I32).rearrange("p (j s w) -> p s j w", j=GROUP_CAPS, s=SLOTS),
         )
-        w_planes = []
-        for a in range(GROUPS):
-            planes = by_group.tile([P, PASSES, GROUP_COLS], U8, align_bytes=64)
-            nc.vector.tensor_copy(
-                out=planes[:].rearrange("p g c -> p (g c)").bitcast(I32).rearrange(
-                    "p (g j w) -> p g j w", g=PASSES, j=GROUP_CAPS
-                ),
-                in_=scales_in_words[:, a],
-            )
-            w_planes.append(planes)
 
         stores = []
         for a in range(GROUPS):
@@ -118,14 +118,15 @@ def tile_capsulelayer_e_kernel(tc, x, W_words, W_scales, out):
                 acc_h = sums.tile([P, GROUP_CAPS, C_OUT], F32)
                 acc.append(acc_h)
             for g in range(PASSES):
+                slot, shared_i = divmod(a * PASSES + g, SHARED)
                 for h in range(HALVES):
                     rows = slice(h * P, (h + 1) * P)
                     nc.tensor.matmul_mx(
                         out=acc[h][:].rearrange("p j o -> p (j o)"),
                         lhsT=x_codes[g][:, rows].bitcast(FP8X4),
                         lhsT_scale=x_planes[g][:, rows],
-                        rhs=w_words[a][:, g].rearrange("p j c -> p (j c)").bitcast(FP8X4),
-                        rhs_scale=w_planes[a][:, g, :],
+                        rhs=w_words[a * PASSES + g][:].rearrange("p j c -> p (j c)").bitcast(FP8X4),
+                        rhs_scale=w_planes[4 * shared_i : P, slot, :],
                         start=(g == 0),
                         stop=(g == PASSES - 1),
                     )
@@ -153,7 +154,7 @@ def tile_capsulelayer_e_kernel(tc, x, W_words, W_scales, out):
                     in1=factor[:, h, :].unsqueeze(2).to_broadcast([P, GROUP_CAPS, C_OUT]),
                     op=ALU.mult,
                 )
-                stores.append((out_rows[h][:, a * GROUP_CAPS : (a + 1) * GROUP_CAPS, :], v))
+                stores.append((out_rows[h][:, a:CAPS:GROUPS, :], v))
 
         for rows_of_out, v in stores:
             nc.sync.dma_start(out=rows_of_out, in_=v[:])

@@ -15,19 +15,23 @@ BATCH, ROUTES, C_IN, CAPS, C_OUT = 256, 1152, 8, 16, 16
 K = ROUTES * C_IN
 P = 128
 PACK = 4
+BLOCK = 32
 K_PASS = P * PACK
 PASSES = K // K_PASS
+STEPS = 2
 HALVES = BATCH // P
 GROUPS = 2
 GROUP_CAPS = CAPS // GROUPS
 GROUP_COLS = GROUP_CAPS * C_OUT
+ROW_BYTES = C_OUT * PACK
 PAIRS = PACK // 2
+PASS_PAIRS = K_PASS // 2
 CHUNK_PASSES = 3
 CHUNKS = PASSES // CHUNK_PASSES
 CHUNK_K = CHUNK_PASSES * K_PASS
-BLOCKS = K_PASS // 32
+CHUNK_BLOCKS = CHUNK_K // BLOCK
+BLOCKS = K_PASS // BLOCK
 SCALE_WORDS = C_OUT // 4
-ROWS_PER_CHUNK = -(-BLOCKS // CHUNKS)
 SHARED = 4
 SLOTS = GROUPS * PASSES // SHARED
 
@@ -37,21 +41,21 @@ FLOPS = 2 * BATCH * K * CAPS * C_OUT
 def tile_capsulelayer_e_kernel(tc, x, W_words, W_scales, out):
     nc = tc.nc
     x_rows = x.rearrange("(h b) r i -> b h (r i)", b=P)
-    w_by_pass = W_words.rearrange("(j a g) p o t -> a g p j (o t)", a=GROUPS, g=PASSES)
+    w_by_pass = W_words.rearrange(
+        "(j a g) (m n) o t -> a g m j (n o t)", a=GROUPS, g=PASSES, n=STEPS
+    )
     scale_rows = W_scales.rearrange("(s i) q o -> q i s o", i=SHARED)
     out_rows = out.rearrange("e (h b) y z o -> h b e (y z o)", b=P)
 
     with tc.manual_schedule(), tc.tile_pool(name="keep", bufs=1) as keep, tc.tile_pool(
         name="x_in", bufs=CHUNKS
-    ) as x_in, tc.tile_pool(name="by_pass", bufs=PASSES) as by_pass, tc.tile_pool(
+    ) as x_in, tc.tile_pool(name="x_mx", bufs=STEPS * PASSES) as x_mx, tc.tile_pool(
         name="by_group", bufs=GROUPS
     ) as by_group, tc.tile_pool(name="operands", bufs=GROUPS * PASSES) as operands, tc.tile_pool(
         name="stage", bufs=3
-    ) as stage, tc.tile_pool(
-        name="results", bufs=GROUPS * HALVES
-    ) as results, tc.psum_pool(name="flipped", bufs=4) as flipped, tc.psum_pool(
-        name="sums", bufs=GROUPS * HALVES
-    ) as sums:
+    ) as stage, tc.tile_pool(name="results", bufs=GROUPS * HALVES) as results, tc.psum_pool(
+        name="flipped", bufs=4
+    ) as flipped, tc.psum_pool(name="sums", bufs=GROUPS * HALVES) as sums:
         w_scales_in = keep.tile([P, CAPS * PASSES // SHARED * C_OUT], U8, align_bytes=64)
         nc.vector.memset(w_scales_in[:].bitcast(I32), 0)
         one = keep.tile([P, 1], F32)
@@ -60,48 +64,55 @@ def tile_capsulelayer_e_kernel(tc, x, W_words, W_scales, out):
         nc.scalar.activation(out=warm[:], in_=one[:], func=ACT.Sqrt)
         ident = keep.tile([P, P], F32)
         masks.make_identity(nc, ident[:])
+        w_landed = keep.tile([P, GROUPS * PASSES, GROUP_CAPS, STEPS * ROW_BYTES], U8, align_bytes=64)
+        nc.vector.memset(w_landed[:].rearrange("p n j c -> p (n j c)").bitcast(I32), 0)
 
         x_chunks = []
         for c in range(CHUNKS):
-            x_sb = x_in.tile([P, HALVES, CHUNK_K], BF16)
-            nc.scalar.dma_start(out=x_sb[:], in_=x_rows[:, :, c * CHUNK_K : (c + 1) * CHUNK_K])
+            x_sb = x_in.tile([P, HALVES, CHUNK_K + BLOCK], BF16)
+            nc.sync.dma_start(out=x_sb[:, :, 0:CHUNK_K], in_=x_rows[:, :, c * CHUNK_K : (c + 1) * CHUNK_K])
             x_chunks.append(x_sb)
-            for q in range(c * ROWS_PER_CHUNK, min((c + 1) * ROWS_PER_CHUNK, BLOCKS)):
-                row = 32 * (q // 4) + q % 4
-                nc.sync.dma_start(
-                    out=w_scales_in[row : row + 4 * SHARED : 4, :].bitcast(I32).rearrange(
-                        "i (s w) -> i s w", w=SCALE_WORDS
-                    ),
-                    in_=scale_rows[q].bitcast(I32),
-                )
-        w_words = []
+        for q in range(BLOCKS):
+            row = 32 * (q // 4) + q % 4
+            nc.sync.dma_start(
+                out=w_scales_in[row : row + 4 * SHARED : 4, :].bitcast(I32).rearrange(
+                    "i (s w) -> i s w", w=SCALE_WORDS
+                ),
+                in_=scale_rows[q].bitcast(I32),
+            )
         for a in range(GROUPS):
             for g in range(PASSES):
-                w_sb = operands.tile([P, GROUP_CAPS, C_OUT * PACK], U8, align_bytes=64)
-                nc.sync.dma_start(out=w_sb[:].bitcast(I32), in_=w_by_pass[a, g].bitcast(I32))
-                w_words.append(w_sb)
+                nc.sync.dma_start(
+                    out=w_landed[0:P:STEPS, a * PASSES + g].bitcast(I32), in_=w_by_pass[a, g].bitcast(I32)
+                )
 
-        x_codes = []
-        x_planes = []
-        for g in range(PASSES):
-            x_pairs = x_chunks[g // CHUNK_PASSES][:].bitcast(F32)
-            first = (g % CHUNK_PASSES) * (K_PASS // 2)
+        def flip_and_quantise(x_pairs, first):
             x_t = flipped.tile([P, HALVES, PAIRS, P], F32)
             for h in range(HALVES):
                 for u in range(PAIRS):
-                    nc.tensor.transpose(
-                        x_t[:, h, u, :], x_pairs[:, h, first + u : first + K_PASS // 2 : PAIRS], ident[:]
-                    )
+                    nc.tensor.transpose(x_t[:, h, u, :], x_pairs[:, h, first + u : first + PASS_PAIRS : PAIRS], ident[:])
             grouped = stage.tile([P, BATCH * PACK], BF16, align_bytes=64)
             nc.scalar.copy(
                 out=grouped[:].bitcast(F32).rearrange("p (h b u) -> p h b u", h=HALVES, u=PAIRS),
                 in_=x_t[:].rearrange("p h u b -> p h b u"),
             )
-            codes = by_pass.tile([P, BATCH], U32, align_bytes=64)
-            plane = by_pass.tile([P, BATCH], U8, align_bytes=64)
+            codes = x_mx.tile([P, BATCH], U32, align_bytes=64)
+            plane = x_mx.tile([P, BATCH], U8, align_bytes=64)
             nc.vector.quantize_mx(out=codes[:].bitcast(FP8X4), scales=plane[:], in_=grouped[:])
-            x_codes.append(codes)
-            x_planes.append(plane)
+            return codes, plane
+
+        x_steps = [[], []]
+        for c in range(CHUNKS + 1):
+            if c < CHUNKS:
+                for n in range(CHUNK_PASSES):
+                    x_steps[0].append(flip_and_quantise(x_chunks[c][:].bitcast(F32), n * PASS_PAIRS))
+                blocks = x_chunks[c][:].rearrange("p h (n v) -> p h n v", v=BLOCK)
+                heads = stage.tile([P, HALVES, CHUNK_BLOCKS, PACK], BF16)
+                nc.vector.tensor_copy(out=heads[:], in_=blocks[:, :, 0:CHUNK_BLOCKS, 0:PACK])
+                nc.vector.tensor_copy(out=blocks[:, :, 1 : CHUNK_BLOCKS + 1, 0:PACK], in_=heads[:])
+            if c > 0:
+                for n in range(CHUNK_PASSES):
+                    x_steps[1].append(flip_and_quantise(x_chunks[c - 1][:].bitcast(F32), n * PASS_PAIRS + PAIRS))
 
         w_planes = keep.tile([P, SLOTS, GROUP_COLS], U8, align_bytes=64)
         nc.vector.tensor_copy(
@@ -119,17 +130,24 @@ def tile_capsulelayer_e_kernel(tc, x, W_words, W_scales, out):
                 acc.append(acc_h)
             for g in range(PASSES):
                 slot, shared_i = divmod(a * PASSES + g, SHARED)
-                for h in range(HALVES):
-                    rows = slice(h * P, (h + 1) * P)
-                    nc.tensor.matmul_mx(
-                        out=acc[h][:].rearrange("p j o -> p (j o)"),
-                        lhsT=x_codes[g][:, rows].bitcast(FP8X4),
-                        lhsT_scale=x_planes[g][:, rows],
-                        rhs=w_words[a * PASSES + g][:].rearrange("p j c -> p (j c)").bitcast(FP8X4),
-                        rhs_scale=w_planes[4 * shared_i : P, slot, :],
-                        start=(g == 0),
-                        stop=(g == PASSES - 1),
-                    )
+                w_op = operands.tile([P, STEPS, GROUP_CAPS, ROW_BYTES], U8, align_bytes=64)
+                nc.vector.tensor_copy(
+                    out=w_op[:].bitcast(I32),
+                    in_=w_landed[:, a * PASSES + g].bitcast(I32).rearrange("p j (n w) -> p n j w", n=STEPS),
+                )
+                for n in range(STEPS):
+                    codes, plane = x_steps[n][g]
+                    for h in range(HALVES):
+                        rows = slice(h * P, (h + 1) * P)
+                        nc.tensor.matmul_mx(
+                            out=acc[h][:].rearrange("p j o -> p (j o)"),
+                            lhsT=codes[:, rows].bitcast(FP8X4),
+                            lhsT_scale=plane[:, rows],
+                            rhs=w_op[:, n].rearrange("p j c -> p (j c)").bitcast(FP8X4),
+                            rhs_scale=w_planes[4 * shared_i : P, slot, :],
+                            start=(g == 0 and n == 0),
+                            stop=(g == PASSES - 1 and n == STEPS - 1),
+                        )
 
             squares = by_group.tile([P, HALVES, GROUP_CAPS, C_OUT], F32)
             sq = by_group.tile([P, HALVES, GROUP_CAPS], F32)

@@ -32,8 +32,14 @@ CHUNK_K = CHUNK_PASSES * K_PASS
 CHUNK_BLOCKS = CHUNK_K // BLOCK
 BLOCKS = K_PASS // BLOCK
 SCALE_WORDS = C_OUT // 4
+QUADRANT = 32
+QUADRANT_BLOCKS = QUADRANT * PACK // BLOCK
 SHARED = 4
 SLOTS = GROUPS * PASSES // SHARED
+LANDINGS = 6
+PARTS = GROUPS * HALVES
+FLIP_BANKS = 8 - PARTS
+STAGE_BUFS = 3
 
 FLOPS = 2 * BATCH * K * CAPS * C_OUT
 
@@ -41,21 +47,19 @@ FLOPS = 2 * BATCH * K * CAPS * C_OUT
 def tile_capsulelayer_e_kernel(tc, x, W_words, W_scales, out):
     nc = tc.nc
     x_rows = x.rearrange("(h b) r i -> b h (r i)", b=P)
-    w_by_pass = W_words.rearrange(
-        "(j a g) (m n) o t -> a g m j (n o t)", a=GROUPS, g=PASSES, n=STEPS
-    )
+    w_by_pass = W_words.rearrange("(e g) (m n) o t -> g m e (n o t)", g=PASSES, n=STEPS)
     scale_rows = W_scales.rearrange("(s i) q o -> q i s o", i=SHARED)
     out_rows = out.rearrange("e (h b) y z o -> h b e (y z o)", b=P)
 
     with tc.manual_schedule(), tc.tile_pool(name="keep", bufs=1) as keep, tc.tile_pool(
         name="x_in", bufs=CHUNKS
     ) as x_in, tc.tile_pool(name="x_mx", bufs=STEPS * PASSES) as x_mx, tc.tile_pool(
-        name="by_group", bufs=GROUPS
-    ) as by_group, tc.tile_pool(name="operands", bufs=GROUPS * PASSES) as operands, tc.tile_pool(
-        name="stage", bufs=3
-    ) as stage, tc.tile_pool(name="results", bufs=GROUPS * HALVES) as results, tc.psum_pool(
-        name="flipped", bufs=4
-    ) as flipped, tc.psum_pool(name="sums", bufs=GROUPS * HALVES) as sums:
+        name="operands", bufs=PASSES
+    ) as operands, tc.tile_pool(name="stage", bufs=STAGE_BUFS) as stage, tc.tile_pool(
+        name="results", bufs=PARTS
+    ) as results, tc.psum_pool(name="flipped", bufs=FLIP_BANKS) as flipped, tc.psum_pool(
+        name="sums", bufs=PARTS
+    ) as sums:
         w_scales_in = keep.tile([P, CAPS * PASSES // SHARED * C_OUT], U8, align_bytes=64)
         nc.vector.memset(w_scales_in[:].bitcast(I32), 0)
         one = keep.tile([P, 1], F32)
@@ -64,8 +68,8 @@ def tile_capsulelayer_e_kernel(tc, x, W_words, W_scales, out):
         nc.scalar.activation(out=warm[:], in_=one[:], func=ACT.Sqrt)
         ident = keep.tile([P, P], F32)
         masks.make_identity(nc, ident[:])
-        w_landed = keep.tile([P, GROUPS * PASSES, GROUP_CAPS, STEPS * ROW_BYTES], U8, align_bytes=64)
-        nc.vector.memset(w_landed[:].rearrange("p n j c -> p (n j c)").bitcast(I32), 0)
+        w_landed = keep.tile([P, LANDINGS, CAPS, STEPS * ROW_BYTES], U8, align_bytes=64)
+        nc.vector.memset(w_landed[:].rearrange("p g e c -> p (g e c)").bitcast(I32), 0)
 
         x_chunks = []
         for c in range(CHUNKS):
@@ -73,18 +77,18 @@ def tile_capsulelayer_e_kernel(tc, x, W_words, W_scales, out):
             nc.sync.dma_start(out=x_sb[:, :, 0:CHUNK_K], in_=x_rows[:, :, c * CHUNK_K : (c + 1) * CHUNK_K])
             x_chunks.append(x_sb)
         for q in range(BLOCKS):
-            row = 32 * (q // 4) + q % 4
+            row = QUADRANT * (q // QUADRANT_BLOCKS) + q % QUADRANT_BLOCKS
             nc.sync.dma_start(
-                out=w_scales_in[row : row + 4 * SHARED : 4, :].bitcast(I32).rearrange(
+                out=w_scales_in[row : row + QUADRANT_BLOCKS * SHARED : QUADRANT_BLOCKS, :].bitcast(I32).rearrange(
                     "i (s w) -> i s w", w=SCALE_WORDS
                 ),
                 in_=scale_rows[q].bitcast(I32),
             )
-        for a in range(GROUPS):
-            for g in range(PASSES):
-                nc.sync.dma_start(
-                    out=w_landed[0:P:STEPS, a * PASSES + g].bitcast(I32), in_=w_by_pass[a, g].bitcast(I32)
-                )
+        def load_w(g):
+            nc.sync.dma_start(out=w_landed[0:P:STEPS, g % LANDINGS].bitcast(I32), in_=w_by_pass[g].bitcast(I32))
+
+        for g in range(LANDINGS):
+            load_w(g)
 
         def flip_and_quantise(x_pairs, first):
             x_t = flipped.tile([P, HALVES, PAIRS, P], F32)
@@ -101,18 +105,18 @@ def tile_capsulelayer_e_kernel(tc, x, W_words, W_scales, out):
             nc.vector.quantize_mx(out=codes[:].bitcast(FP8X4), scales=plane[:], in_=grouped[:])
             return codes, plane
 
-        x_steps = [[], []]
+        x_steps = [[] for step in range(STEPS)]
         for c in range(CHUNKS + 1):
             if c < CHUNKS:
-                for n in range(CHUNK_PASSES):
-                    x_steps[0].append(flip_and_quantise(x_chunks[c][:].bitcast(F32), n * PASS_PAIRS))
-                blocks = x_chunks[c][:].rearrange("p h (n v) -> p h n v", v=BLOCK)
-                heads = stage.tile([P, HALVES, CHUNK_BLOCKS, PACK], BF16)
-                nc.vector.tensor_copy(out=heads[:], in_=blocks[:, :, 0:CHUNK_BLOCKS, 0:PACK])
-                nc.vector.tensor_copy(out=blocks[:, :, 1 : CHUNK_BLOCKS + 1, 0:PACK], in_=heads[:])
+                for local in range(CHUNK_PASSES):
+                    x_steps[0].append(flip_and_quantise(x_chunks[c][:].bitcast(F32), local * PASS_PAIRS))
+                blocks = x_chunks[c][:].bitcast(F32).rearrange("p h (n v) -> p h n v", v=BLOCK // 2)
+                heads = stage.tile([P, HALVES, CHUNK_BLOCKS, PAIRS], F32)
+                nc.vector.tensor_copy(out=heads[:], in_=blocks[:, :, 0:CHUNK_BLOCKS, 0:PAIRS])
+                nc.vector.tensor_copy(out=blocks[:, :, 1 : CHUNK_BLOCKS + 1, 0:PAIRS], in_=heads[:])
             if c > 0:
-                for n in range(CHUNK_PASSES):
-                    x_steps[1].append(flip_and_quantise(x_chunks[c - 1][:].bitcast(F32), n * PASS_PAIRS + PAIRS))
+                for local in range(CHUNK_PASSES):
+                    x_steps[1].append(flip_and_quantise(x_chunks[c - 1][:].bitcast(F32), local * PASS_PAIRS + PAIRS))
 
         w_planes = keep.tile([P, SLOTS, GROUP_COLS], U8, align_bytes=64)
         nc.vector.tensor_copy(
@@ -122,57 +126,58 @@ def tile_capsulelayer_e_kernel(tc, x, W_words, W_scales, out):
             in_=w_scales_in[:].bitcast(I32).rearrange("p (j s w) -> p s j w", j=GROUP_CAPS, s=SLOTS),
         )
 
-        stores = []
+        acc = []
         for a in range(GROUPS):
-            acc = []
             for h in range(HALVES):
-                acc_h = sums.tile([P, GROUP_CAPS, C_OUT], F32)
-                acc.append(acc_h)
-            for g in range(PASSES):
+                acc_ah = sums.tile([P, GROUP_CAPS, C_OUT], F32)
+                acc.append(acc_ah)
+        for g in range(PASSES):
+            w_op = operands.tile([P, GROUPS, STEPS, GROUP_CAPS, ROW_BYTES], U8, align_bytes=64)
+            nc.vector.tensor_copy(
+                out=w_op[:].bitcast(I32),
+                in_=w_landed[:, g % LANDINGS].bitcast(I32).rearrange("p (j a) (n w) -> p a n j w", a=GROUPS, n=STEPS),
+            )
+            if g + LANDINGS < PASSES:
+                load_w(g + LANDINGS)
+            for a in range(GROUPS):
                 slot, shared_i = divmod(a * PASSES + g, SHARED)
-                w_op = operands.tile([P, STEPS, GROUP_CAPS, ROW_BYTES], U8, align_bytes=64)
-                nc.vector.tensor_copy(
-                    out=w_op[:].bitcast(I32),
-                    in_=w_landed[:, a * PASSES + g].bitcast(I32).rearrange("p j (n w) -> p n j w", n=STEPS),
-                )
-                for n in range(STEPS):
-                    codes, plane = x_steps[n][g]
+                for step in range(STEPS):
+                    codes, plane = x_steps[step][g]
                     for h in range(HALVES):
                         rows = slice(h * P, (h + 1) * P)
                         nc.tensor.matmul_mx(
-                            out=acc[h][:].rearrange("p j o -> p (j o)"),
+                            out=acc[a * HALVES + h][:].rearrange("p j o -> p (j o)"),
                             lhsT=codes[:, rows].bitcast(FP8X4),
                             lhsT_scale=plane[:, rows],
-                            rhs=w_op[:, n].rearrange("p j c -> p (j c)").bitcast(FP8X4),
-                            rhs_scale=w_planes[4 * shared_i : P, slot, :],
-                            start=(g == 0 and n == 0),
-                            stop=(g == PASSES - 1 and n == STEPS - 1),
+                            rhs=w_op[:, a, step].rearrange("p j c -> p (j c)").bitcast(FP8X4),
+                            rhs_scale=w_planes[QUADRANT_BLOCKS * shared_i : P, slot, :],
+                            start=(g == 0 and step == 0),
+                            stop=(g == PASSES - 1 and step == STEPS - 1),
                         )
 
-            squares = by_group.tile([P, HALVES, GROUP_CAPS, C_OUT], F32)
-            sq = by_group.tile([P, HALVES, GROUP_CAPS], F32)
+        squares = keep.tile([P, PARTS, GROUP_CAPS, C_OUT], F32)
+        sq = keep.tile([P, PARTS, GROUP_CAPS], F32)
+        for part in range(PARTS):
+            nc.scalar.activation(out=squares[:, part], in_=acc[part][:], func=ACT.Square, scale=1.0 / ROUTES)
+            nc.vector.tensor_reduce(out=sq[:, part, :], in_=squares[:, part], axis=AXIS.X, op=ALU.add)
+        root = keep.tile([P, PARTS, GROUP_CAPS], F32)
+        nc.scalar.activation(out=root[:], in_=sq[:], func=ACT.Sqrt)
+        one_plus_sq = keep.tile([P, PARTS, GROUP_CAPS], F32)
+        nc.vector.tensor_scalar_add(one_plus_sq[:], sq[:], 1.0)
+        inverse = keep.tile([P, PARTS, GROUP_CAPS], F32)
+        nc.vector.reciprocal(inverse[:], one_plus_sq[:])
+        factor = keep.tile([P, PARTS, GROUP_CAPS], F32)
+        nc.vector.scalar_tensor_tensor(
+            out=factor[:], in0=root[:], scalar=1.0 / ROUTES, in1=inverse[:], op0=ALU.mult, op1=ALU.mult
+        )
+        for a in range(GROUPS):
             for h in range(HALVES):
-                nc.scalar.activation(out=squares[:, h], in_=acc[h][:], func=ACT.Square, scale=1.0 / ROUTES)
-                nc.vector.tensor_reduce(out=sq[:, h, :], in_=squares[:, h], axis=AXIS.X, op=ALU.add)
-            root = by_group.tile([P, HALVES, GROUP_CAPS], F32)
-            nc.scalar.activation(out=root[:], in_=sq[:], func=ACT.Sqrt)
-            one_plus_sq = by_group.tile([P, HALVES, GROUP_CAPS], F32)
-            nc.vector.tensor_scalar_add(one_plus_sq[:], sq[:], 1.0)
-            inverse = by_group.tile([P, HALVES, GROUP_CAPS], F32)
-            nc.vector.reciprocal(inverse[:], one_plus_sq[:])
-            factor = by_group.tile([P, HALVES, GROUP_CAPS], F32)
-            nc.vector.scalar_tensor_tensor(
-                out=factor[:], in0=root[:], scalar=1.0 / ROUTES, in1=inverse[:], op0=ALU.mult, op1=ALU.mult
-            )
-            for h in range(HALVES):
+                part = a * HALVES + h
                 v = results.tile([P, GROUP_CAPS, C_OUT], F32)
                 nc.vector.tensor_tensor(
                     out=v[:],
-                    in0=acc[h][:],
-                    in1=factor[:, h, :].unsqueeze(2).to_broadcast([P, GROUP_CAPS, C_OUT]),
+                    in0=acc[part][:],
+                    in1=factor[:, part, :].unsqueeze(2).to_broadcast([P, GROUP_CAPS, C_OUT]),
                     op=ALU.mult,
                 )
-                stores.append((out_rows[h][:, a:CAPS:GROUPS, :], v))
-
-        for rows_of_out, v in stores:
-            nc.sync.dma_start(out=rows_of_out, in_=v[:])
+                nc.sync.dma_start(out=out_rows[h][:, a:CAPS:GROUPS, :], in_=v[:])

import concourse.masks as masks
import concourse.mybir as mybir

F32 = mybir.dt.float32
BF16 = mybir.dt.bfloat16
I32 = mybir.dt.int32
U32 = mybir.dt.uint32
U8 = mybir.dt.uint8
FP8X4 = mybir.dt.float8_e4m3fn_x4
ACT = mybir.ActivationFunctionType
ALU = mybir.AluOpType
AXIS = mybir.AxisListType

BATCH, ROUTES, C_IN, CAPS, C_OUT = 256, 1152, 8, 16, 16
K = ROUTES * C_IN
P = 128
PACK = 4
BLOCK = 32
K_PASS = P * PACK
PASSES = K // K_PASS
STEPS = 2
HALVES = BATCH // P
GROUPS = 2
GROUP_CAPS = CAPS // GROUPS
GROUP_COLS = GROUP_CAPS * C_OUT
ROW_BYTES = C_OUT * PACK
PAIRS = PACK // 2
PASS_PAIRS = K_PASS // 2
CHUNK_PASSES = 3
CHUNKS = PASSES // CHUNK_PASSES
CHUNK_K = CHUNK_PASSES * K_PASS
CHUNK_BLOCKS = CHUNK_K // BLOCK
BLOCKS = K_PASS // BLOCK
SCALE_WORDS = C_OUT // 4
QUADRANT = 32
QUADRANT_BLOCKS = QUADRANT * PACK // BLOCK
SHARED = 4
SLOTS = GROUPS * PASSES // SHARED
LANDINGS = 6
PARTS = GROUPS * HALVES
FLIP_BANKS = 8 - PARTS
STAGE_BUFS = 3

FLOPS = 2 * BATCH * K * CAPS * C_OUT


def tile_capsulelayer_e_kernel(tc, x, W_words, W_scales, out):
    nc = tc.nc
    x_rows = x.rearrange("(h b) r i -> b h (r i)", b=P)
    w_by_pass = W_words.rearrange("(e g) (m n) o t -> g m e (n o t)", g=PASSES, n=STEPS)
    scale_rows = W_scales.rearrange("(s i) q o -> q i s o", i=SHARED)
    out_rows = out.rearrange("e (h b) y z o -> h b e (y z o)", b=P)

    with tc.manual_schedule(), tc.tile_pool(name="keep", bufs=1) as keep, tc.tile_pool(
        name="x_in", bufs=CHUNKS
    ) as x_in, tc.tile_pool(name="x_mx", bufs=STEPS * PASSES) as x_mx, tc.tile_pool(
        name="operands", bufs=PASSES
    ) as operands, tc.tile_pool(name="stage", bufs=STAGE_BUFS) as stage, tc.tile_pool(
        name="results", bufs=PARTS
    ) as results, tc.psum_pool(name="flipped", bufs=FLIP_BANKS) as flipped, tc.psum_pool(
        name="sums", bufs=PARTS
    ) as sums:
        w_scales_in = keep.tile([P, CAPS * PASSES // SHARED * C_OUT], U8, align_bytes=64)
        nc.vector.memset(w_scales_in[:].bitcast(I32), 0)
        one = keep.tile([P, 1], F32)
        nc.vector.memset(one[:], 1.0)
        warm = keep.tile([P, 1], F32)
        nc.scalar.activation(out=warm[:], in_=one[:], func=ACT.Sqrt)
        ident = keep.tile([P, P], F32)
        masks.make_identity(nc, ident[:])
        w_landed = keep.tile([P, LANDINGS, CAPS, STEPS * ROW_BYTES], U8, align_bytes=64)
        nc.vector.memset(w_landed[:].rearrange("p g e c -> p (g e c)").bitcast(I32), 0)

        x_chunks = []
        for c in range(CHUNKS):
            x_sb = x_in.tile([P, HALVES, CHUNK_K + BLOCK], BF16)
            nc.sync.dma_start(out=x_sb[:, :, 0:CHUNK_K], in_=x_rows[:, :, c * CHUNK_K : (c + 1) * CHUNK_K])
            x_chunks.append(x_sb)
        for q in range(BLOCKS):
            row = QUADRANT * (q // QUADRANT_BLOCKS) + q % QUADRANT_BLOCKS
            nc.sync.dma_start(
                out=w_scales_in[row : row + QUADRANT_BLOCKS * SHARED : QUADRANT_BLOCKS, :].bitcast(I32).rearrange(
                    "i (s w) -> i s w", w=SCALE_WORDS
                ),
                in_=scale_rows[q].bitcast(I32),
            )
        def load_w(g):
            nc.sync.dma_start(out=w_landed[0:P:STEPS, g % LANDINGS].bitcast(I32), in_=w_by_pass[g].bitcast(I32))

        for g in range(LANDINGS):
            load_w(g)

        def flip_and_quantise(x_pairs, first):
            x_t = flipped.tile([P, HALVES, PAIRS, P], F32)
            for h in range(HALVES):
                for u in range(PAIRS):
                    nc.tensor.transpose(x_t[:, h, u, :], x_pairs[:, h, first + u : first + PASS_PAIRS : PAIRS], ident[:])
            grouped = stage.tile([P, BATCH * PACK], BF16, align_bytes=64)
            nc.scalar.copy(
                out=grouped[:].bitcast(F32).rearrange("p (h b u) -> p h b u", h=HALVES, u=PAIRS),
                in_=x_t[:].rearrange("p h u b -> p h b u"),
            )
            codes = x_mx.tile([P, BATCH], U32, align_bytes=64)
            plane = x_mx.tile([P, BATCH], U8, align_bytes=64)
            nc.vector.quantize_mx(out=codes[:].bitcast(FP8X4), scales=plane[:], in_=grouped[:])
            return codes, plane

        x_steps = [[] for step in range(STEPS)]
        for c in range(CHUNKS + 1):
            if c < CHUNKS:
                for local in range(CHUNK_PASSES):
                    x_steps[0].append(flip_and_quantise(x_chunks[c][:].bitcast(F32), local * PASS_PAIRS))
                blocks = x_chunks[c][:].bitcast(F32).rearrange("p h (n v) -> p h n v", v=BLOCK // 2)
                heads = stage.tile([P, HALVES, CHUNK_BLOCKS, PAIRS], F32)
                nc.vector.tensor_copy(out=heads[:], in_=blocks[:, :, 0:CHUNK_BLOCKS, 0:PAIRS])
                nc.vector.tensor_copy(out=blocks[:, :, 1 : CHUNK_BLOCKS + 1, 0:PAIRS], in_=heads[:])
            if c > 0:
                for local in range(CHUNK_PASSES):
                    x_steps[1].append(flip_and_quantise(x_chunks[c - 1][:].bitcast(F32), local * PASS_PAIRS + PAIRS))

        w_planes = keep.tile([P, SLOTS, GROUP_COLS], U8, align_bytes=64)
        nc.vector.tensor_copy(
            out=w_planes[:].rearrange("p s c -> p (s c)").bitcast(I32).rearrange(
                "p (s j w) -> p s j w", s=SLOTS, j=GROUP_CAPS
            ),
            in_=w_scales_in[:].bitcast(I32).rearrange("p (j s w) -> p s j w", j=GROUP_CAPS, s=SLOTS),
        )

        acc = []
        for a in range(GROUPS):
            for h in range(HALVES):
                acc_ah = sums.tile([P, GROUP_CAPS, C_OUT], F32)
                acc.append(acc_ah)
        for g in range(PASSES):
            w_op = operands.tile([P, GROUPS, STEPS, GROUP_CAPS, ROW_BYTES], U8, align_bytes=64)
            nc.vector.tensor_copy(
                out=w_op[:].bitcast(I32),
                in_=w_landed[:, g % LANDINGS].bitcast(I32).rearrange("p (j a) (n w) -> p a n j w", a=GROUPS, n=STEPS),
            )
            if g + LANDINGS < PASSES:
                load_w(g + LANDINGS)
            for a in range(GROUPS):
                slot, shared_i = divmod(a * PASSES + g, SHARED)
                for step in range(STEPS):
                    codes, plane = x_steps[step][g]
                    for h in range(HALVES):
                        rows = slice(h * P, (h + 1) * P)
                        nc.tensor.matmul_mx(
                            out=acc[a * HALVES + h][:].rearrange("p j o -> p (j o)"),
                            lhsT=codes[:, rows].bitcast(FP8X4),
                            lhsT_scale=plane[:, rows],
                            rhs=w_op[:, a, step].rearrange("p j c -> p (j c)").bitcast(FP8X4),
                            rhs_scale=w_planes[QUADRANT_BLOCKS * shared_i : P, slot, :],
                            start=(g == 0 and step == 0),
                            stop=(g == PASSES - 1 and step == STEPS - 1),
                        )

        squares = keep.tile([P, PARTS, GROUP_CAPS, C_OUT], F32)
        sq = keep.tile([P, PARTS, GROUP_CAPS], F32)
        for part in range(PARTS):
            nc.scalar.activation(out=squares[:, part], in_=acc[part][:], func=ACT.Square, scale=1.0 / ROUTES)
            nc.vector.tensor_reduce(out=sq[:, part, :], in_=squares[:, part], axis=AXIS.X, op=ALU.add)
        root = keep.tile([P, PARTS, GROUP_CAPS], F32)
        nc.scalar.activation(out=root[:], in_=sq[:], func=ACT.Sqrt)
        one_plus_sq = keep.tile([P, PARTS, GROUP_CAPS], F32)
        nc.vector.tensor_scalar_add(one_plus_sq[:], sq[:], 1.0)
        inverse = keep.tile([P, PARTS, GROUP_CAPS], F32)
        nc.vector.reciprocal(inverse[:], one_plus_sq[:])
        factor = keep.tile([P, PARTS, GROUP_CAPS], F32)
        nc.vector.scalar_tensor_tensor(
            out=factor[:], in0=root[:], scalar=1.0 / ROUTES, in1=inverse[:], op0=ALU.mult, op1=ALU.mult
        )
        for a in range(GROUPS):
            for h in range(HALVES):
                part = a * HALVES + h
                v = results.tile([P, GROUP_CAPS, C_OUT], F32)
                nc.vector.tensor_tensor(
                    out=v[:],
                    in0=acc[part][:],
                    in1=factor[:, part, :].unsqueeze(2).to_broadcast([P, GROUP_CAPS, C_OUT]),
                    op=ALU.mult,
                )
                nc.sync.dma_start(out=out_rows[h][:, a:CAPS:GROUPS, :], in_=v[:])
